import numpy as np
import ml_dtypes


def mxq(x, axis, fmt="e4m3"):
    dtype, down = {"e4m3": (ml_dtypes.float8_e4m3fn, 7), "e5m2": (ml_dtypes.float8_e5m2, 14)}[fmt]
    v = np.moveaxis(np.asarray(x, np.float32).astype(ml_dtypes.bfloat16).astype(np.float64), axis, -1)
    blocks = v.reshape(v.shape[:-1] + (-1, 32))
    amax = np.abs(blocks).max(-1, keepdims=True)
    byte = np.maximum(np.where(amax > 0, np.frexp(amax)[1] - 1 + 127, 0) - down, 1)
    scale = np.exp2(byte - 127.0)
    codes = (blocks / scale).astype(np.float32).astype(dtype).astype(np.float64)
    return np.moveaxis((codes * scale).reshape(v.shape), -1, axis)


WIDE = False


def mx_kscale(k):
    if not WIDE:
        return np.ones(k)
    levels = np.array([10, -10, 5, -5, 0])
    a = np.random.permutation(np.resize(levels, k // 512 * 4)).reshape(k // 512, 4)
    idx = np.arange(k)
    return np.exp2(a[idx // 512, idx % 128 // 32])


BF16 = ml_dtypes.bfloat16


def bf(x):
    return np.asarray(x, np.float32).astype(BF16)


def f64(x):
    return np.asarray(x).astype(np.float64)


B, M, N, P = 6, 1024, 1024, 512
EPS = 1e-05


def normalize(v, axes, gamma, beta):
    mean = v.mean(axis=axes, keepdims=True)
    std = np.sqrt(v.var(axis=axes, keepdims=True, ddof=1))
    return gamma * ((v - mean) / (std + EPS)) + beta


def setup_inputs():
    s = mx_kscale(N)
    return {"x": bf(np.random.standard_normal((B, M, N)) * s),
            "original_xj_y": bf(np.random.standard_normal((N, P)) * 0.5 / np.sqrt(N) / s[:, None]),
            "original_xi_y": bf(np.random.standard_normal((M, P)) * 2.0 / np.sqrt(M)),
            "gamma_o_sum": bf(1.0 + 0.1 * np.random.standard_normal(P)),
            "gamma_o": bf(1.0 + 0.1 * np.random.standard_normal((P, P))),
            "beta_o_sum": bf(0.1 * np.random.standard_normal(P)),
            "beta_o": bf(0.1 * np.random.standard_normal((P, P)))}


def reference(x, original_xj_y, original_xi_y, gamma_o_sum, gamma_o, beta_o_sum, beta_o):
    oyy = mxq(f64(x), 2, "e4m3") @ mxq(f64(original_xj_y), 0, "e4m3")
    o_sum = normalize(oyy.sum(axis=-2), (-1,), f64(gamma_o_sum), f64(beta_o_sum)) + 1.0
    oyy = mxq(np.swapaxes(oyy, -1, -2), 2, "e4m3") @ mxq(f64(original_xi_y), 0, "e4m3")
    oyy = np.swapaxes(oyy, -1, -2)
    oyy = normalize(oyy, (-2, -1), f64(gamma_o), f64(beta_o))
    return oyy, o_sum

@@ -1,0 +1,389 @@
+from contextlib import ExitStack
+
+import concourse.mybir as mybir
+from concourse.masks import make_identity
+
+F32 = mybir.dt.float32
+BF16 = mybir.dt.bfloat16
+U32 = mybir.dt.uint32
+U8 = mybir.dt.uint8
+FP8X4 = mybir.dt.float8_e4m3fn_x4
+ACT = mybir.ActivationFunctionType
+ALU = mybir.AluOpType
+AXIS = mybir.AxisListType
+
+BATCH = 6
+ROWS = 1024
+INNER = 1024
+WIDTH = 512
+EPS = 1e-05
+
+P = 128
+PACK = 4
+K_PASS = P * PACK
+PASSES = 2
+BANK = 512
+TILES = WIDTH // P
+HALVES = BATCH * PASSES
+X_AHEAD = 6
+FIRST_LOAD_PIECES = 4
+
+SECOND_MATMUL_STEP = 2
+MEAN_STEP = 3
+STD_STEP = 4
+BIAS_STEP = 5
+LAST_STEP = BIAS_STEP + 2 * (BATCH - 1)
+
+FLOPS = BATCH * (2 * ROWS * INNER * WIDTH + 2 * ROWS * WIDTH * WIDTH)
+
+
+def batch_at(step, first_step):
+    b, rest = divmod(step - first_step, PASSES)
+    return b if rest == 0 and 0 <= b < BATCH else None
+
+
+def tile_selfprojection_pa_kernel(
+    tc,
+    x,
+    original_xj_y,
+    original_xi_y,
+    gamma_o_sum,
+    gamma_o,
+    beta_o_sum,
+    beta_o,
+    out_0,
+    out_1,
+):
+    nc = tc.nc
+    with ExitStack() as ctx:
+        consts = ctx.enter_context(tc.tile_pool(name="consts", bufs=1))
+        weights = ctx.enter_context(tc.tile_pool(name="weights", bufs=2))
+        x_pool = ctx.enter_context(tc.tile_pool(name="x_pool", bufs=X_AHEAD))
+        work = ctx.enter_context(tc.tile_pool(name="work", bufs=2))
+        small = ctx.enter_context(tc.tile_pool(name="small", bufs=2))
+        psum = ctx.enter_context(tc.psum_pool(name="psum", bufs=8))
+        ctx.enter_context(tc.manual_schedule())
+
+        def load_x_half(h, pieces):
+            b, g = divmod(h, PASSES)
+            x_half = x_pool.tile([P, PACK * INNER], BF16)
+            row_groups = x[b].rearrange("(g p t) n -> g p t n", g=PASSES, p=P, t=PACK)
+            in_sbuf = x_half[:].rearrange("p (t n) -> p t n", t=PACK)
+            per_piece = PACK // pieces
+            for first in range(0, PACK, per_piece):
+                nc.sync.dma_start(
+                    out=in_sbuf[:, first : first + per_piece, :],
+                    in_=row_groups[g][:, first : first + per_piece, :],
+                )
+            return x_half
+
+        def load_weight(in_word_order):
+            raw = weights.tile([P, PASSES * PACK * WIDTH], BF16)
+            for s in range(PASSES):
+                nc.sync.dma_start(
+                    out=raw[:, s * PACK * WIDTH : (s + 1) * PACK * WIDTH].rearrange(
+                        "p (u e w) -> p u e w", u=2, e=2
+                    ),
+                    in_=in_word_order[s],
+                )
+            return raw
+
+        xj_raw = load_weight(
+            original_xj_y.rearrange("(c u q e) j -> c q u e j", c=PASSES, u=2, q=P, e=2)
+        )
+        x_halves = {0: load_x_half(0, FIRST_LOAD_PIECES), 1: load_x_half(1, 1)}
+        xi_raw = load_weight(
+            original_xi_y.rearrange("(g p u e) i -> g p u e i", g=PASSES, p=P, u=2, e=2)
+        )
+        x_halves[2] = load_x_half(2, 1)
+        gamma = consts.tile([P, TILES * WIDTH], BF16)
+        nc.sync.dma_start(
+            out=gamma[:].rearrange("p (it j) -> p it j", it=TILES),
+            in_=gamma_o.rearrange("(it p) j -> p it j", p=P),
+        )
+        beta = consts.tile([P, TILES * WIDTH], BF16)
+        nc.sync.dma_start(
+            out=beta[:].rearrange("p (it j) -> p it j", it=TILES),
+            in_=beta_o.rearrange("(it p) j -> p it j", p=P),
+        )
+        for h in range(3, X_AHEAD):
+            x_halves[h] = load_x_half(h, 1)
+        gamma_sum = consts.tile([P, WIDTH], BF16)
+        nc.sync.dma_start(out=gamma_sum[0:BATCH, :], in_=gamma_o_sum.partition_broadcast(BATCH))
+        beta_sum = consts.tile([P, WIDTH], BF16)
+        nc.sync.dma_start(out=beta_sum[0:BATCH, :], in_=beta_o_sum.partition_broadcast(BATCH))
+
+        identity = consts.tile([P, P], F32)
+        make_identity(nc, identity[:])
+        ones = consts.tile([P, P], F32)
+        nc.gpsimd.memset(ones[:], 1.0)
+        neg_average = consts.tile([P, P], F32)
+        nc.gpsimd.memset(neg_average[:], -1.0 / (WIDTH * WIDTH))
+        selectors = consts.tile([P, BATCH * P], F32)
+        nc.gpsimd.memset(selectors[:], 0.0)
+        for b in range(BATCH):
+            nc.gpsimd.memset(selectors[:, b * P + b : b * P + b + 1], 1.0)
+        one = consts.tile([P, 1], F32)
+        nc.vector.memset(one[:], 1.0)
+        sqrt_of_one = consts.tile([P, 1], F32)
+        nc.scalar.activation(out=sqrt_of_one[:], in_=one[:], func=ACT.Sqrt)
+
+        def quantise_weight(raw, codes, scales):
+            grouped = weights.tile([P, PASSES * PACK * WIDTH], BF16, align_bytes=64)
+            for s in range(PASSES):
+                cols = slice(s * PACK * WIDTH, (s + 1) * PACK * WIDTH)
+                nc.vector.tensor_copy(
+                    out=grouped[:, cols].rearrange("p (w i t) -> p w t i", i=4, t=PACK),
+                    in_=raw[:, cols].rearrange("p (t w i) -> p w t i", t=PACK, i=4),
+                )
+            nc.vector.quantize_mx(out=codes[:].bitcast(FP8X4), scales=scales[:], in_=grouped[:])
+
+        xj_codes = consts.tile([P, PASSES * WIDTH], U32, align_bytes=64)
+        xj_scales = consts.tile([P, PASSES * WIDTH], U8, align_bytes=64)
+        xi_codes = consts.tile([P, PASSES * WIDTH], U32, align_bytes=64)
+        xi_scales = consts.tile([P, PASSES * WIDTH], U8, align_bytes=64)
+
+        def transpose_x_rows(x_half, t, x_grouped):
+            words = x_half[:].bitcast(F32)
+            bank = psum.tile([P, BANK], F32, tag="bank")
+            for cu in range(BANK // P):
+                first = t * (INNER // 2) + cu * P
+                nc.tensor.transpose(
+                    bank[:, cu * P : (cu + 1) * P], words[:, first : first + P], identity[:]
+                )
+            grouped_words = x_grouped[:].bitcast(F32).rearrange(
+                "q (c t m u) -> q c t m u", c=PASSES, t=PACK, m=P, u=2
+            )
+            nc.scalar.copy(
+                out=grouped_words[:, :, t, :, :],
+                in_=bank[:].rearrange("q (c u m) -> q c m u", c=PASSES, u=2, m=P),
+            )
+
+        def quantise_x(x_grouped):
+            x_codes = work.tile([P, PASSES * PACK * P], U32, align_bytes=64)
+            x_scales = work.tile([P, PASSES * PACK * P], U8, align_bytes=64)
+            nc.vector.quantize_mx(
+                out=x_codes[:].bitcast(FP8X4), scales=x_scales[:], in_=x_grouped[:]
+            )
+            return x_codes, x_scales
+
+        def first_matmul(jc, x_codes, x_scales, y_grouped, half_sums):
+            bank = psum.tile([P, BANK], F32, tag="bank")
+            for t in range(PACK):
+                for c in range(PASSES):
+                    m_cols = slice((c * PACK + t) * P, (c * PACK + t + 1) * P)
+                    j_cols = slice(c * WIDTH + jc * P, c * WIDTH + (jc + 1) * P)
+                    nc.tensor.matmul_mx(
+                        out=bank[:, t * P : (t + 1) * P],
+                        lhsT=x_codes[:, m_cols].bitcast(FP8X4),
+                        lhsT_scale=x_scales[:, m_cols],
+                        rhs=xj_codes[:, j_cols].bitcast(FP8X4),
+                        rhs_scale=xj_scales[:, j_cols],
+                        start=(c == 0),
+                        stop=(c == PASSES - 1),
+                    )
+            by_column = bank[:].rearrange("p (t j) -> p j t", t=PACK)
+            nc.scalar.copy(
+                out=y_grouped[:, jc * BANK : (jc + 1) * BANK].rearrange(
+                    "p (j t) -> p j t", t=PACK
+                ),
+                in_=by_column,
+            )
+            nc.vector.tensor_reduce(
+                out=half_sums[:, jc * P : (jc + 1) * P], in_=by_column, axis=AXIS.X, op=ALU.add
+            )
+
+        def second_matmul(it, y_codes, y_scales, z, row_sums):
+            bank = psum.tile([P, BANK], F32, tag="bank")
+            for g in range(PASSES):
+                i_cols = slice(g * WIDTH + it * P, g * WIDTH + (it + 1) * P)
+                j_cols = slice(g * WIDTH, (g + 1) * WIDTH)
+                nc.tensor.matmul_mx(
+                    out=bank[:],
+                    lhsT=xi_codes[:, i_cols].bitcast(FP8X4),
+                    lhsT_scale=xi_scales[:, i_cols],
+                    rhs=y_codes[:, j_cols].bitcast(FP8X4),
+                    rhs_scale=y_scales[:, j_cols],
+                    start=(g == 0),
+                    stop=(g == PASSES - 1),
+                )
+            nc.scalar.activation(
+                out=z[:, it * WIDTH : (it + 1) * WIDTH],
+                in_=bank[:],
+                func=ACT.Copy,
+                accum_out=row_sums[:, it : it + 1],
+            )
+
+        def total_over_partitions(weight, parts, total):
+            bank = psum.tile([P, BANK], F32, tag="bank")
+            nc.tensor.matmul(
+                out=bank[:, 0:TILES], lhsT=weight[:], rhs=parts[:], start=True, stop=True
+            )
+            nc.vector.tensor_reduce(out=total[:], in_=bank[:, 0:TILES], axis=AXIS.X, op=ALU.add)
+
+        def one_over_std(rows, sum_or_variance, scale):
+            std = small.tile([P, 1], F32)
+            nc.scalar.activation(
+                out=std[rows, :], in_=sum_or_variance, func=ACT.Sqrt, scale=scale
+            )
+            std_eps = small.tile([P, 1], F32)
+            nc.vector.tensor_scalar_add(out=std_eps[rows, :], in0=std[rows, :], scalar1=EPS)
+            inverse = small.tile([P, 1], F32)
+            nc.vector.reciprocal(out=inverse[rows, :], in_=std_eps[rows, :])
+            return inverse
+
+        quantise_weight(xj_raw, xj_codes, xj_scales)
+        all_rows = slice(0, P)
+        c_bank = psum.tile([P, BANK], F32, tag="bank")
+        x_mx = {}
+        y_mx = {}
+        column_sums = {}
+        z = {}
+        row_sums = {}
+        neg_mean = {}
+        square_sums = {}
+        scaled = {}
+        inverse_std = {}
+        for step in range(-1, LAST_STEP + 1):
+            b_second = batch_at(step, SECOND_MATMUL_STEP)
+            b_mean = batch_at(step, MEAN_STEP)
+            b_std = batch_at(step, STD_STEP)
+            b_bias = batch_at(step, BIAS_STEP)
+            coming = step + 1
+
+            if coming < HALVES:
+                x_grouped = work.tile([P, PASSES * PACK * P * PACK], BF16, align_bytes=64)
+                for t in range(PACK):
+                    transpose_x_rows(x_halves[coming], t, x_grouped)
+                if coming + X_AHEAD < HALVES:
+                    x_halves[coming + X_AHEAD] = load_x_half(coming + X_AHEAD, 1)
+
+            if step == 1:
+                quantise_weight(xi_raw, xi_codes, xi_scales)
+            if b_std is not None:
+                gained = work.tile([P, TILES * WIDTH], F32)
+                scaled[b_std] = gained
+            for it in range(TILES):
+                cols = slice(it * WIDTH, (it + 1) * WIDTH)
+                if b_std is not None:
+                    nc.vector.scalar_tensor_tensor(
+                        out=scaled[b_std][:, cols],
+                        in0=z[b_std][:, cols],
+                        scalar=neg_mean[b_std][:],
+                        in1=gamma[:, cols],
+                        op0=ALU.add,
+                        op1=ALU.mult,
+                    )
+                if b_bias is not None:
+                    nc.vector.scalar_tensor_tensor(
+                        out=scaled[b_bias][:, cols],
+                        in0=scaled[b_bias][:, cols],
+                        scalar=inverse_std[b_bias][:],
+                        in1=beta[:, cols],
+                        op0=ALU.mult,
+                        op1=ALU.add,
+                    )
+                    nc.sync.dma_start(
+                        out=out_0[b_bias, it * P : (it + 1) * P, :], in_=scaled[b_bias][:, cols]
+                    )
+                if it == 0:
+                    if b_mean is not None:
+                        minus_mean = small.tile([P, 1], F32)
+                        total_over_partitions(neg_average, row_sums[b_mean], minus_mean)
+                        neg_mean[b_mean] = minus_mean
+                    if b_std is not None:
+                        square_total = small.tile([P, 1], F32)
+                        total_over_partitions(ones, square_sums[b_std], square_total)
+
+            if coming < HALVES:
+                x_mx[coming] = quantise_x(x_grouped)
+
+            if 0 <= step < HALVES:
+                b, g = divmod(step, PASSES)
+                if g == 0:
+                    y_codes = work.tile([P, PASSES * WIDTH], U32, align_bytes=64)
+                    y_scales = work.tile([P, PASSES * WIDTH], U8, align_bytes=64)
+                    y_mx[b] = (y_codes, y_scales)
+                    sums = work.tile([P, PASSES * WIDTH], F32)
+                    column_sums[b] = sums
+                pass_cols = slice(g * WIDTH, (g + 1) * WIDTH)
+                y_grouped = work.tile([P, WIDTH * PACK], BF16, align_bytes=64)
+                for jc in range(TILES):
+                    first_matmul(jc, *x_mx[step], y_grouped, column_sums[b][:, pass_cols])
+
+            if b_std is not None:
+                inverse_std[b_std] = one_over_std(
+                    all_rows, square_total[:], 1.0 / (WIDTH * WIDTH - 1)
+                )
+
+            if 0 <= step < HALVES:
+                nc.vector.quantize_mx(
+                    out=y_mx[b][0][:, pass_cols].bitcast(FP8X4),
+                    scales=y_mx[b][1][:, pass_cols],
+                    in_=y_grouped[:],
+                )
+
+            if b_second is not None:
+                z_tile = work.tile([P, TILES * WIDTH], F32)
+                z[b_second] = z_tile
+                z_row_sums = small.tile([P, TILES], F32)
+                row_sums[b_second] = z_row_sums
+                for it in range(TILES):
+                    second_matmul(it, *y_mx[b_second], z_tile, z_row_sums)
+
+            if b_mean is not None:
+                squares = work.tile([P, TILES * WIDTH], BF16)
+                z_square_sums = small.tile([P, TILES], F32)
+                square_sums[b_mean] = z_square_sums
+                for it in range(TILES):
+                    cols = slice(it * WIDTH, (it + 1) * WIDTH)
+                    nc.scalar.activation(
+                        out=squares[:, cols],
+                        in_=z[b_mean][:, cols],
+                        func=ACT.Square,
+                        bias=neg_mean[b_mean][:],
+                        accum_out=z_square_sums[:, it : it + 1],
+                    )
+                batch_sums = work.tile([P, WIDTH], F32)
+                nc.gpsimd.tensor_tensor(
+                    out=batch_sums[:],
+                    in0=column_sums[b_mean][:, 0:WIDTH],
+                    in1=column_sums[b_mean][:, WIDTH : 2 * WIDTH],
+                    op=ALU.add,
+                )
+                nc.tensor.matmul(
+                    out=c_bank[:],
+                    lhsT=selectors[:, b_mean * P : (b_mean + 1) * P],
+                    rhs=batch_sums[:],
+                    start=(b_mean == 0),
+                    stop=(b_mean == BATCH - 1),
+                )
+
+        rows = slice(0, BATCH)
+        beta_sum_plus_1 = consts.tile([P, WIDTH], F32)
+        nc.vector.tensor_scalar_add(
+            out=beta_sum_plus_1[rows, :], in0=beta_sum[rows, :], scalar1=1.0
+        )
+        c_stats = small.tile([P, 6], F32)
+        nc.vector.bn_stats(out=c_stats[rows, :], in_=c_bank[rows, :])
+        mean_var = small.tile([P, 2], F32)
+        nc.vector.bn_aggr(out=mean_var[rows, :], in_=c_stats[rows, :])
+        c_inverse_std = one_over_std(rows, mean_var[rows, 1:2], WIDTH / (WIDTH - 1.0))
+        o_sum = work.tile([P, WIDTH], F32)
+        nc.vector.scalar_tensor_tensor(
+            out=o_sum[rows, :],
+            in0=c_bank[rows, :],
+            scalar=mean_var[rows, 0:1],
+            in1=gamma_sum[rows, :],
+            op0=ALU.subtract,
+            op1=ALU.mult,
+        )
+        nc.vector.scalar_tensor_tensor(
+            out=o_sum[rows, :],
+            in0=o_sum[rows, :],
+            scalar=c_inverse_std[rows, :],
+            in1=beta_sum_plus_1[rows, :],
+            op0=ALU.mult,
+            op1=ALU.add,
+        )
+        nc.sync.dma_start(out=out_1[:, :], in_=o_sum[rows, :])

@@ -27,6 +27,8 @@ TILES = WIDTH // P
 HALVES = BATCH * PASSES
 X_AHEAD = 6
 FIRST_LOAD_PIECES = 4
+PIECES = 2
+PIECE = TILES * WIDTH // PIECES
 
 SECOND_MATMUL_STEP = 2
 MEAN_STEP = 3
@@ -95,6 +97,10 @@ def tile_selfprojection_pa_kernel(
         xi_raw = load_weight(
             original_xi_y.rearrange("(g p u e) i -> g p u e i", g=PASSES, p=P, u=2, e=2)
         )
+        gamma_sum = consts.tile([P, WIDTH], BF16)
+        nc.sync.dma_start(out=gamma_sum[0:BATCH, :], in_=gamma_o_sum.partition_broadcast(BATCH))
+        beta_sum = consts.tile([P, WIDTH], BF16)
+        nc.sync.dma_start(out=beta_sum[0:BATCH, :], in_=beta_o_sum.partition_broadcast(BATCH))
         x_halves[2] = load_x_half(2, 1)
         gamma = consts.tile([P, TILES * WIDTH], BF16)
         nc.sync.dma_start(
@@ -108,10 +114,6 @@ def tile_selfprojection_pa_kernel(
         )
         for h in range(3, X_AHEAD):
             x_halves[h] = load_x_half(h, 1)
-        gamma_sum = consts.tile([P, WIDTH], BF16)
-        nc.sync.dma_start(out=gamma_sum[0:BATCH, :], in_=gamma_o_sum.partition_broadcast(BATCH))
-        beta_sum = consts.tile([P, WIDTH], BF16)
-        nc.sync.dma_start(out=beta_sum[0:BATCH, :], in_=beta_o_sum.partition_broadcast(BATCH))
 
         identity = consts.tile([P, P], F32)
         make_identity(nc, identity[:])
@@ -216,10 +218,9 @@ def tile_selfprojection_pa_kernel(
 
         def total_over_partitions(weight, parts, total):
             bank = psum.tile([P, BANK], F32, tag="bank")
-            nc.tensor.matmul(
-                out=bank[:, 0:TILES], lhsT=weight[:], rhs=parts[:], start=True, stop=True
-            )
-            nc.vector.tensor_reduce(out=total[:], in_=bank[:, 0:TILES], axis=AXIS.X, op=ALU.add)
+            totals = bank[:, 0 : parts.shape[1]]
+            nc.tensor.matmul(out=totals, lhsT=weight[:], rhs=parts[:], start=True, stop=True)
+            nc.vector.tensor_reduce(out=total[:], in_=totals, axis=AXIS.X, op=ALU.add)
 
         def one_over_std(rows, sum_or_variance, scale):
             std = small.tile([P, 1], F32)
@@ -234,6 +235,10 @@ def tile_selfprojection_pa_kernel(
 
         quantise_weight(xj_raw, xj_codes, xj_scales)
         all_rows = slice(0, P)
+        c_rows = slice(0, BATCH)
+        beta_sum_plus_1 = consts.tile([P, WIDTH], F32)
+        c_stats = consts.tile([P, 6], F32)
+        c_mean_var = consts.tile([P, 2], F32)
         c_bank = psum.tile([P, BANK], F32, tag="bank")
         x_mx = {}
         y_mx = {}
@@ -260,11 +265,17 @@ def tile_selfprojection_pa_kernel(
 
             if step == 1:
                 quantise_weight(xi_raw, xi_codes, xi_scales)
+                nc.vector.tensor_scalar_add(
+                    out=beta_sum_plus_1[c_rows, :], in0=beta_sum[c_rows, :], scalar1=1.0
+                )
+            if b_std == BATCH - 1:
+                nc.vector.bn_stats(out=c_stats[c_rows, :], in_=c_bank[c_rows, :])
+                nc.vector.bn_aggr(out=c_mean_var[c_rows, :], in_=c_stats[c_rows, :])
             if b_std is not None:
                 gained = work.tile([P, TILES * WIDTH], F32)
                 scaled[b_std] = gained
-            for it in range(TILES):
-                cols = slice(it * WIDTH, (it + 1) * WIDTH)
+            for piece in range(PIECES):
+                cols = slice(piece * PIECE, (piece + 1) * PIECE)
                 if b_std is not None:
                     nc.vector.scalar_tensor_tensor(
                         out=scaled[b_std][:, cols],
@@ -283,17 +294,18 @@ def tile_selfprojection_pa_kernel(
                         op0=ALU.mult,
                         op1=ALU.add,
                     )
+                    piece_rows = slice(piece * PIECE // WIDTH * P, (piece + 1) * PIECE // WIDTH * P)
                     nc.sync.dma_start(
-                        out=out_0[b_bias, it * P : (it + 1) * P, :], in_=scaled[b_bias][:, cols]
+                        out=out_0[b_bias, piece_rows, :].rearrange("(it p) j -> p it j", p=P),
+                        in_=scaled[b_bias][:, cols].rearrange("p (it j) -> p it j", j=WIDTH),
                     )
-                if it == 0:
-                    if b_mean is not None:
-                        minus_mean = small.tile([P, 1], F32)
-                        total_over_partitions(neg_average, row_sums[b_mean], minus_mean)
-                        neg_mean[b_mean] = minus_mean
-                    if b_std is not None:
-                        square_total = small.tile([P, 1], F32)
-                        total_over_partitions(ones, square_sums[b_std], square_total)
+            if b_mean is not None:
+                minus_mean = small.tile([P, 1], F32)
+                total_over_partitions(neg_average, row_sums[b_mean], minus_mean)
+                neg_mean[b_mean] = minus_mean
+            if b_std is not None:
+                square_total = small.tile([P, 1], F32)
+                total_over_partitions(ones, square_sums[b_std], square_total)
 
             if coming < HALVES:
                 x_mx[coming] = quantise_x(x_grouped)
@@ -333,16 +345,16 @@ def tile_selfprojection_pa_kernel(
 
             if b_mean is not None:
                 squares = work.tile([P, TILES * WIDTH], BF16)
-                z_square_sums = small.tile([P, TILES], F32)
+                z_square_sums = small.tile([P, PIECES], F32)
                 square_sums[b_mean] = z_square_sums
-                for it in range(TILES):
-                    cols = slice(it * WIDTH, (it + 1) * WIDTH)
+                for piece in range(PIECES):
+                    cols = slice(piece * PIECE, (piece + 1) * PIECE)
                     nc.scalar.activation(
                         out=squares[:, cols],
                         in_=z[b_mean][:, cols],
                         func=ACT.Square,
                         bias=neg_mean[b_mean][:],
-                        accum_out=z_square_sums[:, it : it + 1],
+                        accum_out=z_square_sums[:, piece : piece + 1],
                     )
                 batch_sums = work.tile([P, WIDTH], F32)
                 nc.gpsimd.tensor_tensor(
@@ -359,31 +371,22 @@ def tile_selfprojection_pa_kernel(
                     stop=(b_mean == BATCH - 1),
                 )
 
-        rows = slice(0, BATCH)
-        beta_sum_plus_1 = consts.tile([P, WIDTH], F32)
-        nc.vector.tensor_scalar_add(
-            out=beta_sum_plus_1[rows, :], in0=beta_sum[rows, :], scalar1=1.0
-        )
-        c_stats = small.tile([P, 6], F32)
-        nc.vector.bn_stats(out=c_stats[rows, :], in_=c_bank[rows, :])
-        mean_var = small.tile([P, 2], F32)
-        nc.vector.bn_aggr(out=mean_var[rows, :], in_=c_stats[rows, :])
-        c_inverse_std = one_over_std(rows, mean_var[rows, 1:2], WIDTH / (WIDTH - 1.0))
+        c_inverse_std = one_over_std(c_rows, c_mean_var[c_rows, 1:2], WIDTH / (WIDTH - 1.0))
         o_sum = work.tile([P, WIDTH], F32)
         nc.vector.scalar_tensor_tensor(
-            out=o_sum[rows, :],
-            in0=c_bank[rows, :],
-            scalar=mean_var[rows, 0:1],
-            in1=gamma_sum[rows, :],
+            out=o_sum[c_rows, :],
+            in0=c_bank[c_rows, :],
+            scalar=c_mean_var[c_rows, 0:1],
+            in1=gamma_sum[c_rows, :],
             op0=ALU.subtract,
             op1=ALU.mult,
         )
         nc.vector.scalar_tensor_tensor(
-            out=o_sum[rows, :],
-            in0=o_sum[rows, :],
-            scalar=c_inverse_std[rows, :],
-            in1=beta_sum_plus_1[rows, :],
+            out=o_sum[c_rows, :],
+            in0=o_sum[c_rows, :],
+            scalar=c_inverse_std[c_rows, :],
+            in1=beta_sum_plus_1[c_rows, :],
             op0=ALU.mult,
             op1=ALU.add,
         )
-        nc.sync.dma_start(out=out_1[:, :], in_=o_sum[rows, :])
+        nc.sync.dma_start(out=out_1[:, :], in_=o_sum[c_rows, :])

@@ -145,7 +145,7 @@ def tile_selfprojection_pa_kernel(
         xi_codes = consts.tile([P, PASSES * WIDTH], U32, align_bytes=64)
         xi_scales = consts.tile([P, PASSES * WIDTH], U8, align_bytes=64)
 
-        def transpose_x_rows(x_half, t, x_grouped):
+        def transpose_x_rows(x_half, t, x_grouped, copy_on_vector):
             words = x_half[:].bitcast(F32)
             bank = psum.tile([P, BANK], F32, tag="bank")
             for cu in range(BANK // P):
@@ -154,26 +154,31 @@ def tile_selfprojection_pa_kernel(
                     bank[:, cu * P : (cu + 1) * P], words[:, first : first + P], identity[:]
                 )
             grouped_words = x_grouped[:].bitcast(F32).rearrange(
-                "q (c t m u) -> q c t m u", c=PASSES, t=PACK, m=P, u=2
+                "q (t c m u) -> q t c m u", t=PACK, c=PASSES, m=P, u=2
             )
-            nc.scalar.copy(
-                out=grouped_words[:, :, t, :, :],
-                in_=bank[:].rearrange("q (c u m) -> q c m u", c=PASSES, u=2, m=P),
-            )
+            side_by_side = bank[:].rearrange("q (c u m) -> q c m u", c=PASSES, u=2, m=P)
+            if copy_on_vector:
+                nc.vector.tensor_copy(out=grouped_words[:, t, :, :, :], in_=side_by_side)
+            else:
+                nc.scalar.copy(out=grouped_words[:, t, :, :, :], in_=side_by_side)
 
         def quantise_x(x_grouped):
-            x_codes = work.tile([P, PASSES * PACK * P], U32, align_bytes=64)
-            x_scales = work.tile([P, PASSES * PACK * P], U8, align_bytes=64)
-            nc.vector.quantize_mx(
-                out=x_codes[:].bitcast(FP8X4), scales=x_scales[:], in_=x_grouped[:]
-            )
+            x_codes = work.tile([P, PACK * PASSES * P], U32, align_bytes=64)
+            x_scales = work.tile([P, PACK * PASSES * P], U8, align_bytes=64)
+            for t in range(PACK):
+                word_cols = slice(t * PASSES * P, (t + 1) * PASSES * P)
+                nc.vector.quantize_mx(
+                    out=x_codes[:, word_cols].bitcast(FP8X4),
+                    scales=x_scales[:, word_cols],
+                    in_=x_grouped[:, t * PASSES * P * PACK : (t + 1) * PASSES * P * PACK],
+                )
             return x_codes, x_scales
 
         def first_matmul(jc, x_codes, x_scales, y_grouped, half_sums):
             bank = psum.tile([P, BANK], F32, tag="bank")
             for t in range(PACK):
                 for c in range(PASSES):
-                    m_cols = slice((c * PACK + t) * P, (c * PACK + t + 1) * P)
+                    m_cols = slice((t * PASSES + c) * P, (t * PASSES + c + 1) * P)
                     j_cols = slice(c * WIDTH + jc * P, c * WIDTH + (jc + 1) * P)
                     nc.tensor.matmul_mx(
                         out=bank[:, t * P : (t + 1) * P],
@@ -216,11 +221,11 @@ def tile_selfprojection_pa_kernel(
                 accum_out=row_sums[:, it : it + 1],
             )
 
-        def total_over_partitions(weight, parts, total):
+        def totals_over_partitions(weight, parts):
             bank = psum.tile([P, BANK], F32, tag="bank")
             totals = bank[:, 0 : parts.shape[1]]
             nc.tensor.matmul(out=totals, lhsT=weight[:], rhs=parts[:], start=True, stop=True)
-            nc.vector.tensor_reduce(out=total[:], in_=totals, axis=AXIS.X, op=ALU.add)
+            return totals
 
         def one_over_std(rows, sum_or_variance, scale):
             std = small.tile([P, 1], F32)
@@ -259,7 +264,7 @@ def tile_selfprojection_pa_kernel(
             if coming < HALVES:
                 x_grouped = work.tile([P, PASSES * PACK * P * PACK], BF16, align_bytes=64)
                 for t in range(PACK):
-                    transpose_x_rows(x_halves[coming], t, x_grouped)
+                    transpose_x_rows(x_halves[coming], t, x_grouped, t == 0 and step % 2 == 0)
                 if coming + X_AHEAD < HALVES:
                     x_halves[coming + X_AHEAD] = load_x_half(coming + X_AHEAD, 1)
 
@@ -268,9 +273,6 @@ def tile_selfprojection_pa_kernel(
                 nc.vector.tensor_scalar_add(
                     out=beta_sum_plus_1[c_rows, :], in0=beta_sum[c_rows, :], scalar1=1.0
                 )
-            if b_std == BATCH - 1:
-                nc.vector.bn_stats(out=c_stats[c_rows, :], in_=c_bank[c_rows, :])
-                nc.vector.bn_aggr(out=c_mean_var[c_rows, :], in_=c_stats[c_rows, :])
             if b_std is not None:
                 gained = work.tile([P, TILES * WIDTH], F32)
                 scaled[b_std] = gained
@@ -299,13 +301,21 @@ def tile_selfprojection_pa_kernel(
                         out=out_0[b_bias, piece_rows, :].rearrange("(it p) j -> p it j", p=P),
                         in_=scaled[b_bias][:, cols].rearrange("p (it j) -> p it j", j=WIDTH),
                     )
+            if b_std == BATCH - 1:
+                nc.vector.bn_stats(out=c_stats[c_rows, :], in_=c_bank[c_rows, :])
+                nc.vector.bn_aggr(out=c_mean_var[c_rows, :], in_=c_stats[c_rows, :])
             if b_mean is not None:
                 minus_mean = small.tile([P, 1], F32)
-                total_over_partitions(neg_average, row_sums[b_mean], minus_mean)
+                tile_means = small.tile([P, TILES], F32)
+                nc.scalar.activation(
+                    out=tile_means[:],
+                    in_=totals_over_partitions(neg_average, row_sums[b_mean]),
+                    func=ACT.Copy,
+                    accum_out=minus_mean[:],
+                )
                 neg_mean[b_mean] = minus_mean
             if b_std is not None:
-                square_total = small.tile([P, 1], F32)
-                total_over_partitions(ones, square_sums[b_std], square_total)
+                square_total = totals_over_partitions(ones, square_sums[b_std])
 
             if coming < HALVES:
                 x_mx[coming] = quantise_x(x_grouped)
@@ -325,7 +335,7 @@ def tile_selfprojection_pa_kernel(
 
             if b_std is not None:
                 inverse_std[b_std] = one_over_std(
-                    all_rows, square_total[:], 1.0 / (WIDTH * WIDTH - 1)
+                    all_rows, square_total, 1.0 / (WIDTH * WIDTH - 1)
                 )
 
             if 0 <= step < HALVES:
@@ -345,17 +355,15 @@ def tile_selfprojection_pa_kernel(
 
             if b_mean is not None:
                 squares = work.tile([P, TILES * WIDTH], BF16)
-                z_square_sums = small.tile([P, PIECES], F32)
+                z_square_sums = small.tile([P, 1], F32)
                 square_sums[b_mean] = z_square_sums
-                for piece in range(PIECES):
-                    cols = slice(piece * PIECE, (piece + 1) * PIECE)
-                    nc.scalar.activation(
-                        out=squares[:, cols],
-                        in_=z[b_mean][:, cols],
-                        func=ACT.Square,
-                        bias=neg_mean[b_mean][:],
-                        accum_out=z_square_sums[:, piece : piece + 1],
-                    )
+                nc.scalar.activation(
+                    out=squares[:],
+                    in_=z[b_mean][:],
+                    func=ACT.Square,
+                    bias=neg_mean[b_mean][:],
+                    accum_out=z_square_sums[:],
+                )
                 batch_sums = work.tile([P, WIDTH], F32)
                 nc.gpsimd.tensor_tensor(
                     out=batch_sums[:],

@@ -196,9 +196,27 @@ def tile_selfprojection_pa_kernel(
                 ),
                 in_=by_column,
             )
-            nc.vector.tensor_reduce(
-                out=half_sums[:, jc * P : (jc + 1) * P], in_=by_column, axis=AXIS.X, op=ALU.add
-            )
+            if half_sums is not None:
+                nc.vector.tensor_reduce(
+                    out=half_sums[:, jc * P : (jc + 1) * P], in_=by_column, axis=AXIS.X, op=ALU.add
+                )
+
+        def add_rows_in_psum(x_codes, x_scales):
+            bank = psum.tile([P, BANK], F32, tag="bank")
+            for t in range(PACK):
+                for c in range(PASSES):
+                    m_cols = slice((t * PASSES + c) * P, (t * PASSES + c + 1) * P)
+                    j_cols = slice(c * WIDTH, (c + 1) * WIDTH)
+                    nc.tensor.matmul_mx(
+                        out=bank[:],
+                        lhsT=x_codes[:, m_cols].bitcast(FP8X4),
+                        lhsT_scale=x_scales[:, m_cols],
+                        rhs=xj_codes[:, j_cols].bitcast(FP8X4),
+                        rhs_scale=xj_scales[:, j_cols],
+                        start=(t == 0 and c == 0),
+                        stop=(t == PACK - 1 and c == PASSES - 1),
+                    )
+            return bank
 
         def second_matmul(it, y_codes, y_scales, z, row_sums):
             bank = psum.tile([P, BANK], F32, tag="bank")
@@ -248,6 +266,7 @@ def tile_selfprojection_pa_kernel(
         x_mx = {}
         y_mx = {}
         column_sums = {}
+        batch_sums = {}
         z = {}
         row_sums = {}
         neg_mean = {}
@@ -264,7 +283,9 @@ def tile_selfprojection_pa_kernel(
             if coming < HALVES:
                 x_grouped = work.tile([P, PASSES * PACK * P * PACK], BF16, align_bytes=64)
                 for t in range(PACK):
-                    transpose_x_rows(x_halves[coming], t, x_grouped, t == 0 and step % 2 == 0)
+                    transpose_x_rows(
+                        x_halves[coming], t, x_grouped, t == 0 and step % 2 == 1 and step > 0
+                    )
                 if coming + X_AHEAD < HALVES:
                     x_halves[coming + X_AHEAD] = load_x_half(coming + X_AHEAD, 1)
 
@@ -326,12 +347,14 @@ def tile_selfprojection_pa_kernel(
                     y_codes = work.tile([P, PASSES * WIDTH], U32, align_bytes=64)
                     y_scales = work.tile([P, PASSES * WIDTH], U8, align_bytes=64)
                     y_mx[b] = (y_codes, y_scales)
-                    sums = work.tile([P, PASSES * WIDTH], F32)
+                    sums = work.tile([P, WIDTH], F32)
                     column_sums[b] = sums
                 pass_cols = slice(g * WIDTH, (g + 1) * WIDTH)
                 y_grouped = work.tile([P, WIDTH * PACK], BF16, align_bytes=64)
                 for jc in range(TILES):
-                    first_matmul(jc, *x_mx[step], y_grouped, column_sums[b][:, pass_cols])
+                    first_matmul(jc, *x_mx[step], y_grouped, column_sums[b] if g == 0 else None)
+                if g == 1:
+                    second_half_sums = add_rows_in_psum(*x_mx[step])
 
             if b_std is not None:
                 inverse_std[b_std] = one_over_std(
@@ -344,6 +367,15 @@ def tile_selfprojection_pa_kernel(
                     scales=y_mx[b][1][:, pass_cols],
                     in_=y_grouped[:],
                 )
+                if g == 1:
+                    sums_of_batch = work.tile([P, WIDTH], F32)
+                    batch_sums[b] = sums_of_batch
+                    nc.vector.tensor_tensor(
+                        out=sums_of_batch[:],
+                        in0=second_half_sums[:],
+                        in1=column_sums[b][:],
+                        op=ALU.add,
+                    )
 
             if b_second is not None:
                 z_tile = work.tile([P, TILES * WIDTH], F32)
@@ -364,17 +396,10 @@ def tile_selfprojection_pa_kernel(
                     bias=neg_mean[b_mean][:],
                     accum_out=z_square_sums[:],
                 )
-                batch_sums = work.tile([P, WIDTH], F32)
-                nc.gpsimd.tensor_tensor(
-                    out=batch_sums[:],
-                    in0=column_sums[b_mean][:, 0:WIDTH],
-                    in1=column_sums[b_mean][:, WIDTH : 2 * WIDTH],
-                    op=ALU.add,
-                )
                 nc.tensor.matmul(
                     out=c_bank[:],
                     lhsT=selectors[:, b_mean * P : (b_mean + 1) * P],
-                    rhs=batch_sums[:],
+                    rhs=batch_sums[b_mean][:],
                     start=(b_mean == 0),
                     stop=(b_mean == BATCH - 1),
                 )

@@ -63,6 +63,7 @@ def tile_selfprojection_pa_kernel(
         x_pool = ctx.enter_context(tc.tile_pool(name="x_pool", bufs=X_AHEAD))
         work = ctx.enter_context(tc.tile_pool(name="work", bufs=2))
         small = ctx.enter_context(tc.tile_pool(name="small", bufs=2))
+        kept = ctx.enter_context(tc.tile_pool(name="kept", bufs=BATCH))
         psum = ctx.enter_context(tc.psum_pool(name="psum", bufs=8))
         ctx.enter_context(tc.manual_schedule())
 
@@ -256,6 +257,16 @@ def tile_selfprojection_pa_kernel(
             nc.vector.reciprocal(out=inverse[rows, :], in_=std_eps[rows, :])
             return inverse
 
+        def put_on_rows(*items):
+            for b in items:
+                nc.tensor.matmul(
+                    out=c_bank[:],
+                    lhsT=selectors[:, b * P : (b + 1) * P],
+                    rhs=batch_sums[b][:],
+                    start=(b == 0),
+                    stop=(b == BATCH - 1),
+                )
+
         quantise_weight(xj_raw, xj_codes, xj_scales)
         all_rows = slice(0, P)
         c_rows = slice(0, BATCH)
@@ -279,6 +290,9 @@ def tile_selfprojection_pa_kernel(
             b_std = batch_at(step, STD_STEP)
             b_bias = batch_at(step, BIAS_STEP)
             coming = step + 1
+
+            if step == HALVES - 1:
+                put_on_rows(0, 1)
 
             if coming < HALVES:
                 x_grouped = work.tile([P, PASSES * PACK * P * PACK], BF16, align_bytes=64)
@@ -355,6 +369,8 @@ def tile_selfprojection_pa_kernel(
                     first_matmul(jc, *x_mx[step], y_grouped, column_sums[b] if g == 0 else None)
                 if g == 1:
                     second_half_sums = add_rows_in_psum(*x_mx[step])
+                if step == HALVES - 1:
+                    put_on_rows(2, 3)
 
             if b_std is not None:
                 inverse_std[b_std] = one_over_std(
@@ -368,7 +384,7 @@ def tile_selfprojection_pa_kernel(
                     in_=y_grouped[:],
                 )
                 if g == 1:
-                    sums_of_batch = work.tile([P, WIDTH], F32)
+                    sums_of_batch = kept.tile([P, WIDTH], F32)
                     batch_sums[b] = sums_of_batch
                     nc.vector.tensor_tensor(
                         out=sums_of_batch[:],
@@ -396,13 +412,8 @@ def tile_selfprojection_pa_kernel(
                     bias=neg_mean[b_mean][:],
                     accum_out=z_square_sums[:],
                 )
-                nc.tensor.matmul(
-                    out=c_bank[:],
-                    lhsT=selectors[:, b_mean * P : (b_mean + 1) * P],
-                    rhs=batch_sums[b_mean][:],
-                    start=(b_mean == 0),
-                    stop=(b_mean == BATCH - 1),
-                )
+                if b_mean == BATCH - 1:
+                    put_on_rows(4, 5)
 
         c_inverse_std = one_over_std(c_rows, c_mean_var[c_rows, 1:2], WIDTH / (WIDTH - 1.0))
         o_sum = work.tile([P, WIDTH], F32)

@@ -44,6 +44,71 @@ def batch_at(step, first_step):
     return b if rest == 0 and 0 <= b < BATCH else None
 
 
+VEC_X = (1, 3, 5, 7, 9)
+
+
+def program():
+    prog = [("xj",)]
+    last = HALVES - 1
+    for step in range(-1, last):
+        b_second = batch_at(step, SECOND_MATMUL_STEP)
+        b_mean = batch_at(step, MEAN_STEP)
+        b_std = batch_at(step, STD_STEP)
+        coming = step + 1
+        b, g = divmod(step, PASSES)
+        for t in range(PACK):
+            prog.append(("tp", coming, t))
+            prog.append(("to", coming, t, t == 0 and step in VEC_X))
+        if coming + X_AHEAD < HALVES:
+            prog.append(("load", coming + X_AHEAD))
+        if step == 1:
+            prog.append(("xi",))
+        if b_mean is not None:
+            prog.extend([("meanp", b_mean), ("meana", b_mean)])
+        if b_std is not None:
+            prog.append(("stdp", b_std))
+        for t in range(PACK):
+            prog.append(("qx", coming, t, 1))
+        if b_mean is not None:
+            prog.extend([("stt1", b_mean, 0, 2), ("stt1", b_mean, 2, 2)])
+        if step >= 0:
+            for jc in range(TILES):
+                prog.append(("m1p", step, jc))
+                prog.append(("m1o", step, jc, False, g == 0))
+            if g == 1:
+                prog.append(("dup", step, True, True))
+        if b_std is not None:
+            prog.extend([("stda", b_std), ("inv", b_std)])
+        if step >= 0:
+            prog.append(("qy", step))
+            if g == 1:
+                prog.append(("add", b))
+        if b_std is not None:
+            prog.extend([("stt2", b_std, 0, 2), ("stt2", b_std, 2, 2)])
+        if b_second is not None:
+            for it in range(TILES):
+                prog.extend([("m2p", b_second, it), ("m2o", b_second, it)])
+        if b_mean is not None:
+            prog.append(("sq", b_mean))
+    b4, b5 = BATCH - 2, BATCH - 1
+    prog.extend([("m1p", last, jc) for jc in range(TILES)])
+    prog.extend([("meanp", b4), ("meana", b4), ("dup", last, True, True)])
+    prog.extend([("sel", 0), ("sel", 1)])
+    prog.append(("stt1", b4, 0, 2))
+    prog.extend([("m1o", last, jc, False, False) for jc in range(TILES)])
+    prog.extend([("qy", last), ("stt1", b4, 2, 2), ("add", b5)])
+    prog.extend([("m2p", b5, 0), ("m2p", b5, 1), ("sq", b4), ("stdp", b4), ("m2p", b5, 2), ("m2p", b5, 3)])
+    prog.extend([("m2o", b5, 0), ("stda", b4), ("m2o", b5, 1), ("m2o", b5, 2), ("m2o", b5, 3)])
+    prog.extend([("sel", 2), ("sel", 3)])
+    prog.extend([("inv", b4), ("stt2", b4, 0, 2), ("stt2", b4, 2, 2)])
+    prog.extend([("meanp", b5), ("meana", b5), ("sq", b5), ("sel", 4), ("sel", 5)])
+    prog.extend([("stt1", b5, 0, 2), ("stt1", b5, 2, 2)])
+    prog.extend([("stdp", b5), ("stda", b5), ("inv", b5)])
+    prog.extend([("c_stats",), ("c_std",)])
+    prog.extend([("stt2", b5, 0, 2), ("stt2", b5, 2, 2), ("c_out",)])
+    return prog
+
+
 def tile_selfprojection_pa_kernel(
     tc,
     x,
@@ -94,7 +159,11 @@ def tile_selfprojection_pa_kernel(
         xj_raw = load_weight(
             original_xj_y.rearrange("(c u q e) j -> c q u e j", c=PASSES, u=2, q=P, e=2)
         )
-        x_halves = {0: load_x_half(0, FIRST_LOAD_PIECES), 1: load_x_half(1, 1)}
+        x_halves = {
+            0: load_x_half(0, FIRST_LOAD_PIECES),
+            1: load_x_half(1, FIRST_LOAD_PIECES),
+            2: load_x_half(2, 1),
+        }
         xi_raw = load_weight(
             original_xi_y.rearrange("(g p u e) i -> g p u e i", g=PASSES, p=P, u=2, e=2)
         )
@@ -102,7 +171,6 @@ def tile_selfprojection_pa_kernel(
         nc.sync.dma_start(out=gamma_sum[0:BATCH, :], in_=gamma_o_sum.partition_broadcast(BATCH))
         beta_sum = consts.tile([P, WIDTH], BF16)
         nc.sync.dma_start(out=beta_sum[0:BATCH, :], in_=beta_o_sum.partition_broadcast(BATCH))
-        x_halves[2] = load_x_half(2, 1)
         gamma = consts.tile([P, TILES * WIDTH], BF16)
         nc.sync.dma_start(
             out=gamma[:].rearrange("p (it j) -> p it j", it=TILES),
@@ -146,7 +214,7 @@ def tile_selfprojection_pa_kernel(
         xi_codes = consts.tile([P, PASSES * WIDTH], U32, align_bytes=64)
         xi_scales = consts.tile([P, PASSES * WIDTH], U8, align_bytes=64)
 
-        def transpose_x_rows(x_half, t, x_grouped, copy_on_vector):
+        def transpose_x_rows(x_half, t):
             words = x_half[:].bitcast(F32)
             bank = psum.tile([P, BANK], F32, tag="bank")
             for cu in range(BANK // P):
@@ -154,6 +222,9 @@ def tile_selfprojection_pa_kernel(
                 nc.tensor.transpose(
                     bank[:, cu * P : (cu + 1) * P], words[:, first : first + P], identity[:]
                 )
+            return bank
+
+        def copy_x_rows(bank, t, x_grouped, copy_on_vector):
             grouped_words = x_grouped[:].bitcast(F32).rearrange(
                 "q (t c m u) -> q t c m u", t=PACK, c=PASSES, m=P, u=2
             )
@@ -163,19 +234,15 @@ def tile_selfprojection_pa_kernel(
             else:
                 nc.scalar.copy(out=grouped_words[:, t, :, :, :], in_=side_by_side)
 
-        def quantise_x(x_grouped):
-            x_codes = work.tile([P, PACK * PASSES * P], U32, align_bytes=64)
-            x_scales = work.tile([P, PACK * PASSES * P], U8, align_bytes=64)
-            for t in range(PACK):
-                word_cols = slice(t * PASSES * P, (t + 1) * PASSES * P)
-                nc.vector.quantize_mx(
-                    out=x_codes[:, word_cols].bitcast(FP8X4),
-                    scales=x_scales[:, word_cols],
-                    in_=x_grouped[:, t * PASSES * P * PACK : (t + 1) * PASSES * P * PACK],
-                )
-            return x_codes, x_scales
+        def quantise_x_rows(x_grouped, x_codes, x_scales, t_first, t_count):
+            word_cols = slice(t_first * PASSES * P, (t_first + t_count) * PASSES * P)
+            nc.vector.quantize_mx(
+                out=x_codes[:, word_cols].bitcast(FP8X4),
+                scales=x_scales[:, word_cols],
+                in_=x_grouped[:, t_first * PASSES * P * PACK : (t_first + t_count) * PASSES * P * PACK],
+            )
 
-        def first_matmul(jc, x_codes, x_scales, y_grouped, half_sums):
+        def first_matmul(jc, x_codes, x_scales):
             bank = psum.tile([P, BANK], F32, tag="bank")
             for t in range(PACK):
                 for c in range(PASSES):
@@ -190,20 +257,21 @@ def tile_selfprojection_pa_kernel(
                         start=(c == 0),
                         stop=(c == PASSES - 1),
                     )
+            return bank
+
+        def copy_y(bank, jc, y_grouped, half_sums, copy_on_vector):
             by_column = bank[:].rearrange("p (t j) -> p j t", t=PACK)
-            nc.scalar.copy(
-                out=y_grouped[:, jc * BANK : (jc + 1) * BANK].rearrange(
-                    "p (j t) -> p j t", t=PACK
-                ),
-                in_=by_column,
-            )
+            y_out = y_grouped[:, jc * BANK : (jc + 1) * BANK].rearrange("p (j t) -> p j t", t=PACK)
+            if copy_on_vector:
+                nc.vector.tensor_copy(out=y_out, in_=by_column)
+            else:
+                nc.scalar.copy(out=y_out, in_=by_column)
             if half_sums is not None:
                 nc.vector.tensor_reduce(
                     out=half_sums[:, jc * P : (jc + 1) * P], in_=by_column, axis=AXIS.X, op=ALU.add
                 )
 
-        def add_rows_in_psum(x_codes, x_scales):
-            bank = psum.tile([P, BANK], F32, tag="bank")
+        def add_rows_in_psum(bank, opens, closes, x_codes, x_scales):
             for t in range(PACK):
                 for c in range(PASSES):
                     m_cols = slice((t * PASSES + c) * P, (t * PASSES + c + 1) * P)
@@ -214,12 +282,11 @@ def tile_selfprojection_pa_kernel(
                         lhsT_scale=x_scales[:, m_cols],
                         rhs=xj_codes[:, j_cols].bitcast(FP8X4),
                         rhs_scale=xj_scales[:, j_cols],
-                        start=(t == 0 and c == 0),
-                        stop=(t == PACK - 1 and c == PASSES - 1),
+                        start=(opens and t == 0 and c == 0),
+                        stop=(closes and t == PACK - 1 and c == PASSES - 1),
                     )
-            return bank
 
-        def second_matmul(it, y_codes, y_scales, z, row_sums):
+        def second_matmul(it, y_codes, y_scales):
             bank = psum.tile([P, BANK], F32, tag="bank")
             for g in range(PASSES):
                 i_cols = slice(g * WIDTH + it * P, g * WIDTH + (it + 1) * P)
@@ -233,6 +300,9 @@ def tile_selfprojection_pa_kernel(
                     start=(g == 0),
                     stop=(g == PASSES - 1),
                 )
+            return bank
+
+        def copy_z(bank, it, z, row_sums):
             nc.scalar.activation(
                 out=z[:, it * WIDTH : (it + 1) * WIDTH],
                 in_=bank[:],
@@ -246,191 +316,242 @@ def tile_selfprojection_pa_kernel(
             nc.tensor.matmul(out=totals, lhsT=weight[:], rhs=parts[:], start=True, stop=True)
             return totals
 
-        def one_over_std(rows, sum_or_variance, scale):
+        def std_of(rows, sum_or_variance, scale):
             std = small.tile([P, 1], F32)
             nc.scalar.activation(
                 out=std[rows, :], in_=sum_or_variance, func=ACT.Sqrt, scale=scale
             )
+            return std
+
+        def one_over(rows, std):
             std_eps = small.tile([P, 1], F32)
             nc.vector.tensor_scalar_add(out=std_eps[rows, :], in0=std[rows, :], scalar1=EPS)
             inverse = small.tile([P, 1], F32)
             nc.vector.reciprocal(out=inverse[rows, :], in_=std_eps[rows, :])
             return inverse
 
-        def put_on_rows(*items):
-            for b in items:
-                nc.tensor.matmul(
-                    out=c_bank[:],
-                    lhsT=selectors[:, b * P : (b + 1) * P],
-                    rhs=batch_sums[b][:],
-                    start=(b == 0),
-                    stop=(b == BATCH - 1),
-                )
-
-        quantise_weight(xj_raw, xj_codes, xj_scales)
         all_rows = slice(0, P)
         c_rows = slice(0, BATCH)
         beta_sum_plus_1 = consts.tile([P, WIDTH], F32)
-        c_stats = consts.tile([P, 6], F32)
         c_mean_var = consts.tile([P, 2], F32)
         c_bank = psum.tile([P, BANK], F32, tag="bank")
+        x_raw = {}
         x_mx = {}
+        y_raw = {}
         y_mx = {}
         column_sums = {}
+        psum_sums = {}
         batch_sums = {}
         z = {}
         row_sums = {}
         neg_mean = {}
         square_sums = {}
         scaled = {}
+        stds = {}
         inverse_std = {}
-        for step in range(-1, LAST_STEP + 1):
-            b_second = batch_at(step, SECOND_MATMUL_STEP)
-            b_mean = batch_at(step, MEAN_STEP)
-            b_std = batch_at(step, STD_STEP)
-            b_bias = batch_at(step, BIAS_STEP)
-            coming = step + 1
+        selected = []
+        banks = {}
 
-            if step == HALVES - 1:
-                put_on_rows(0, 1)
+        def st_load(h):
+            x_halves[h] = load_x_half(h, 1)
 
-            if coming < HALVES:
+        def st_xj():
+            quantise_weight(xj_raw, xj_codes, xj_scales)
+
+        def st_xi():
+            quantise_weight(xi_raw, xi_codes, xi_scales)
+            nc.vector.tensor_scalar_add(
+                out=beta_sum_plus_1[c_rows, :], in0=beta_sum[c_rows, :], scalar1=1.0
+            )
+
+        def st_tp(h, t):
+            banks["t", h, t] = transpose_x_rows(x_halves[h], t)
+
+        def st_to(h, t, on_vector):
+            if h not in x_raw:
                 x_grouped = work.tile([P, PASSES * PACK * P * PACK], BF16, align_bytes=64)
-                for t in range(PACK):
-                    transpose_x_rows(
-                        x_halves[coming], t, x_grouped, t == 0 and step % 2 == 1 and step > 0
-                    )
-                if coming + X_AHEAD < HALVES:
-                    x_halves[coming + X_AHEAD] = load_x_half(coming + X_AHEAD, 1)
+                x_raw[h] = x_grouped
+            copy_x_rows(banks["t", h, t], t, x_raw[h], on_vector)
 
-            if step == 1:
-                quantise_weight(xi_raw, xi_codes, xi_scales)
-                nc.vector.tensor_scalar_add(
-                    out=beta_sum_plus_1[c_rows, :], in0=beta_sum[c_rows, :], scalar1=1.0
-                )
-            if b_std is not None:
-                gained = work.tile([P, TILES * WIDTH], F32)
-                scaled[b_std] = gained
-            for piece in range(PIECES):
-                cols = slice(piece * PIECE, (piece + 1) * PIECE)
-                if b_std is not None:
-                    nc.vector.scalar_tensor_tensor(
-                        out=scaled[b_std][:, cols],
-                        in0=z[b_std][:, cols],
-                        scalar=neg_mean[b_std][:],
-                        in1=gamma[:, cols],
-                        op0=ALU.add,
-                        op1=ALU.mult,
-                    )
-                if b_bias is not None:
-                    nc.vector.scalar_tensor_tensor(
-                        out=scaled[b_bias][:, cols],
-                        in0=scaled[b_bias][:, cols],
-                        scalar=inverse_std[b_bias][:],
-                        in1=beta[:, cols],
-                        op0=ALU.mult,
-                        op1=ALU.add,
-                    )
-                    piece_rows = slice(piece * PIECE // WIDTH * P, (piece + 1) * PIECE // WIDTH * P)
-                    nc.sync.dma_start(
-                        out=out_0[b_bias, piece_rows, :].rearrange("(it p) j -> p it j", p=P),
-                        in_=scaled[b_bias][:, cols].rearrange("p (it j) -> p it j", j=WIDTH),
-                    )
-            if b_std == BATCH - 1:
-                nc.vector.bn_stats(out=c_stats[c_rows, :], in_=c_bank[c_rows, :])
-                nc.vector.bn_aggr(out=c_mean_var[c_rows, :], in_=c_stats[c_rows, :])
-            if b_mean is not None:
-                minus_mean = small.tile([P, 1], F32)
-                tile_means = small.tile([P, TILES], F32)
-                nc.scalar.activation(
-                    out=tile_means[:],
-                    in_=totals_over_partitions(neg_average, row_sums[b_mean]),
-                    func=ACT.Copy,
-                    accum_out=minus_mean[:],
-                )
-                neg_mean[b_mean] = minus_mean
-            if b_std is not None:
-                square_total = totals_over_partitions(ones, square_sums[b_std])
+        def st_qx(h, t_first, t_count):
+            if h not in x_mx:
+                x_codes = work.tile([P, PACK * PASSES * P], U32, align_bytes=64)
+                x_scales = work.tile([P, PACK * PASSES * P], U8, align_bytes=64)
+                x_mx[h] = (x_codes, x_scales)
+            quantise_x_rows(x_raw[h], x_mx[h][0], x_mx[h][1], t_first, t_count)
 
-            if coming < HALVES:
-                x_mx[coming] = quantise_x(x_grouped)
+        def st_m1p(h, jc):
+            banks["y", h, jc] = first_matmul(jc, x_mx[h][0], x_mx[h][1])
 
-            if 0 <= step < HALVES:
-                b, g = divmod(step, PASSES)
-                if g == 0:
-                    y_codes = work.tile([P, PASSES * WIDTH], U32, align_bytes=64)
-                    y_scales = work.tile([P, PASSES * WIDTH], U8, align_bytes=64)
-                    y_mx[b] = (y_codes, y_scales)
-                    sums = work.tile([P, WIDTH], F32)
-                    column_sums[b] = sums
-                pass_cols = slice(g * WIDTH, (g + 1) * WIDTH)
+        def st_m1o(h, jc, on_vector, reduce_on_vector):
+            b, g = divmod(h, PASSES)
+            if h not in y_raw:
                 y_grouped = work.tile([P, WIDTH * PACK], BF16, align_bytes=64)
-                for jc in range(TILES):
-                    first_matmul(jc, *x_mx[step], y_grouped, column_sums[b] if g == 0 else None)
-                if g == 1:
-                    second_half_sums = add_rows_in_psum(*x_mx[step])
-                if step == HALVES - 1:
-                    put_on_rows(2, 3)
+                y_raw[h] = y_grouped
+            if reduce_on_vector and b not in column_sums:
+                sums = work.tile([P, WIDTH], F32)
+                column_sums[b] = sums
+            copy_y(banks["y", h, jc], jc, y_raw[h], column_sums[b] if reduce_on_vector else None, on_vector)
 
-            if b_std is not None:
-                inverse_std[b_std] = one_over_std(
-                    all_rows, square_total, 1.0 / (WIDTH * WIDTH - 1)
+        def st_dup(h, opens, closes):
+            b = h // PASSES
+            if opens:
+                sum_bank = psum.tile([P, BANK], F32, tag="bank")
+                psum_sums[b] = sum_bank
+            add_rows_in_psum(psum_sums[b], opens, closes, x_mx[h][0], x_mx[h][1])
+
+        def st_add(b):
+            sums_of_batch = kept.tile([P, WIDTH], F32)
+            batch_sums[b] = sums_of_batch
+            if b in column_sums:
+                nc.vector.tensor_tensor(
+                    out=sums_of_batch[:], in0=psum_sums[b][:], in1=column_sums[b][:], op=ALU.add
                 )
+            else:
+                nc.vector.tensor_copy(out=sums_of_batch[:], in_=psum_sums[b][:])
 
-            if 0 <= step < HALVES:
-                nc.vector.quantize_mx(
-                    out=y_mx[b][0][:, pass_cols].bitcast(FP8X4),
-                    scales=y_mx[b][1][:, pass_cols],
-                    in_=y_grouped[:],
-                )
-                if g == 1:
-                    sums_of_batch = kept.tile([P, WIDTH], F32)
-                    batch_sums[b] = sums_of_batch
-                    nc.vector.tensor_tensor(
-                        out=sums_of_batch[:],
-                        in0=second_half_sums[:],
-                        in1=column_sums[b][:],
-                        op=ALU.add,
-                    )
+        def st_qy(h):
+            b, g = divmod(h, PASSES)
+            if b not in y_mx:
+                y_codes = work.tile([P, PASSES * WIDTH], U32, align_bytes=64)
+                y_scales = work.tile([P, PASSES * WIDTH], U8, align_bytes=64)
+                y_mx[b] = (y_codes, y_scales)
+            pass_cols = slice(g * WIDTH, (g + 1) * WIDTH)
+            nc.vector.quantize_mx(
+                out=y_mx[b][0][:, pass_cols].bitcast(FP8X4),
+                scales=y_mx[b][1][:, pass_cols],
+                in_=y_raw[h][:],
+            )
 
-            if b_second is not None:
+        def st_m2p(b, it):
+            banks["z", b, it] = second_matmul(it, y_mx[b][0], y_mx[b][1])
+
+        def st_m2o(b, it):
+            if b not in z:
                 z_tile = work.tile([P, TILES * WIDTH], F32)
-                z[b_second] = z_tile
+                z[b] = z_tile
                 z_row_sums = small.tile([P, TILES], F32)
-                row_sums[b_second] = z_row_sums
-                for it in range(TILES):
-                    second_matmul(it, *y_mx[b_second], z_tile, z_row_sums)
+                row_sums[b] = z_row_sums
+            copy_z(banks["z", b, it], it, z[b], row_sums[b])
 
-            if b_mean is not None:
-                squares = work.tile([P, TILES * WIDTH], BF16)
-                z_square_sums = small.tile([P, 1], F32)
-                square_sums[b_mean] = z_square_sums
-                nc.scalar.activation(
-                    out=squares[:],
-                    in_=z[b_mean][:],
-                    func=ACT.Square,
-                    bias=neg_mean[b_mean][:],
-                    accum_out=z_square_sums[:],
-                )
-                if b_mean == BATCH - 1:
-                    put_on_rows(4, 5)
+        def st_meanp(b):
+            banks["mean", b] = totals_over_partitions(neg_average, row_sums[b])
 
-        c_inverse_std = one_over_std(c_rows, c_mean_var[c_rows, 1:2], WIDTH / (WIDTH - 1.0))
-        o_sum = work.tile([P, WIDTH], F32)
-        nc.vector.scalar_tensor_tensor(
-            out=o_sum[c_rows, :],
-            in0=c_bank[c_rows, :],
-            scalar=c_mean_var[c_rows, 0:1],
-            in1=gamma_sum[c_rows, :],
-            op0=ALU.subtract,
-            op1=ALU.mult,
-        )
-        nc.vector.scalar_tensor_tensor(
-            out=o_sum[c_rows, :],
-            in0=o_sum[c_rows, :],
-            scalar=c_inverse_std[c_rows, :],
-            in1=beta_sum_plus_1[c_rows, :],
-            op0=ALU.mult,
-            op1=ALU.add,
-        )
-        nc.sync.dma_start(out=out_1[:, :], in_=o_sum[c_rows, :])
+        def st_meana(b):
+            minus_mean = small.tile([P, 1], F32)
+            tile_means = small.tile([P, TILES], F32)
+            nc.scalar.activation(
+                out=tile_means[:], in_=banks["mean", b], func=ACT.Copy, accum_out=minus_mean[:]
+            )
+            neg_mean[b] = minus_mean
+
+        def st_sq(b):
+            squares = work.tile([P, TILES * WIDTH], BF16)
+            z_square_sums = small.tile([P, 1], F32)
+            square_sums[b] = z_square_sums
+            nc.scalar.activation(
+                out=squares[:],
+                in_=z[b][:],
+                func=ACT.Square,
+                bias=neg_mean[b][:],
+                accum_out=z_square_sums[:],
+            )
+
+        def st_sel(b):
+            selected.append(b)
+            nc.tensor.matmul(
+                out=c_bank[:],
+                lhsT=selectors[:, b * P : (b + 1) * P],
+                rhs=batch_sums[b][:],
+                start=(len(selected) == 1),
+                stop=(len(selected) == BATCH),
+            )
+
+        def st_stt1(b, first, count):
+            if b not in scaled:
+                gained = work.tile([P, TILES * WIDTH], F32)
+                scaled[b] = gained
+            cols = slice(first * WIDTH, (first + count) * WIDTH)
+            nc.vector.scalar_tensor_tensor(
+                out=scaled[b][:, cols],
+                in0=z[b][:, cols],
+                scalar=neg_mean[b][:],
+                in1=gamma[:, cols],
+                op0=ALU.add,
+                op1=ALU.mult,
+            )
+
+        def st_stdp(b):
+            banks["std", b] = totals_over_partitions(ones, square_sums[b])
+
+        def st_stda(b):
+            stds[b] = std_of(all_rows, banks["std", b], 1.0 / (WIDTH * WIDTH - 1))
+
+        def st_inv(b):
+            inverse_std[b] = one_over(all_rows, stds[b])
+
+        def st_stt2(b, first, count):
+            cols = slice(first * WIDTH, (first + count) * WIDTH)
+            nc.vector.scalar_tensor_tensor(
+                out=scaled[b][:, cols],
+                in0=scaled[b][:, cols],
+                scalar=inverse_std[b][:],
+                in1=beta[:, cols],
+                op0=ALU.mult,
+                op1=ALU.add,
+            )
+            nc.sync.dma_start(
+                out=out_0[b, first * P : (first + count) * P, :].rearrange("(it p) j -> p it j", p=P),
+                in_=scaled[b][:, cols].rearrange("p (it j) -> p it j", j=WIDTH),
+            )
+
+        def st_c_stats():
+            c_junk = work.tile([P, WIDTH], BF16)
+            nc.scalar.activation(
+                out=c_junk[c_rows, :],
+                in_=c_bank[c_rows, :],
+                func=ACT.Copy,
+                scale=-1.0 / WIDTH,
+                accum_out=c_mean_var[c_rows, 0:1],
+            )
+            nc.scalar.activation(
+                out=c_junk[c_rows, :],
+                in_=c_bank[c_rows, :],
+                func=ACT.Square,
+                bias=c_mean_var[c_rows, 0:1],
+                accum_out=c_mean_var[c_rows, 1:2],
+            )
+
+        def st_c_std():
+            stds[BATCH] = std_of(c_rows, c_mean_var[c_rows, 1:2], 1.0 / (WIDTH - 1.0))
+
+        def st_c_out():
+            c_inverse_std = one_over(c_rows, stds[BATCH])
+            o_sum = work.tile([P, WIDTH], F32)
+            nc.vector.scalar_tensor_tensor(
+                out=o_sum[c_rows, :],
+                in0=c_bank[c_rows, :],
+                scalar=c_mean_var[c_rows, 0:1],
+                in1=gamma_sum[c_rows, :],
+                op0=ALU.add,
+                op1=ALU.mult,
+            )
+            nc.vector.scalar_tensor_tensor(
+                out=o_sum[c_rows, :],
+                in0=o_sum[c_rows, :],
+                scalar=c_inverse_std[c_rows, :],
+                in1=beta_sum_plus_1[c_rows, :],
+                op0=ALU.mult,
+                op1=ALU.add,
+            )
+            nc.sync.dma_start(out=out_1[:, :], in_=o_sum[c_rows, :])
+
+        stages = {
+            "load": st_load, "xj": st_xj, "xi": st_xi, "tp": st_tp, "to": st_to, "qx": st_qx,
+            "m1p": st_m1p, "m1o": st_m1o, "dup": st_dup, "add": st_add, "qy": st_qy,
+            "m2p": st_m2p, "m2o": st_m2o, "meanp": st_meanp, "meana": st_meana, "sq": st_sq,
+            "sel": st_sel, "stt1": st_stt1, "stdp": st_stdp, "stda": st_stda, "inv": st_inv,
+            "stt2": st_stt2, "c_stats": st_c_stats, "c_std": st_c_std, "c_out": st_c_out,
+        }
+        for entry in program():
+            stages[entry[0]](*entry[1:])

@@ -44,7 +44,7 @@ def batch_at(step, first_step):
     return b if rest == 0 and 0 <= b < BATCH else None
 
 
-VEC_X = (1, 3, 5, 7, 9)
+VEC_X = (1, 2, 3, 4, 5, 6, 7, 8, 9)
 
 
 def program():
@@ -63,6 +63,8 @@ def program():
             prog.append(("load", coming + X_AHEAD))
         if step == 1:
             prog.append(("xi",))
+        if step == 3:
+            prog.append(("beta_sum",))
         if b_mean is not None:
             prog.extend([("meanp", b_mean), ("meana", b_mean)])
         if b_std is not None:
@@ -167,22 +169,23 @@ def tile_selfprojection_pa_kernel(
         xi_raw = load_weight(
             original_xi_y.rearrange("(g p u e) i -> g p u e i", g=PASSES, p=P, u=2, e=2)
         )
-        gamma_sum = consts.tile([P, WIDTH], BF16)
-        nc.sync.dma_start(out=gamma_sum[0:BATCH, :], in_=gamma_o_sum.partition_broadcast(BATCH))
-        beta_sum = consts.tile([P, WIDTH], BF16)
-        nc.sync.dma_start(out=beta_sum[0:BATCH, :], in_=beta_o_sum.partition_broadcast(BATCH))
+        x_halves[3] = load_x_half(3, 1)
         gamma = consts.tile([P, TILES * WIDTH], BF16)
         nc.sync.dma_start(
             out=gamma[:].rearrange("p (it j) -> p it j", it=TILES),
             in_=gamma_o.rearrange("(it p) j -> p it j", p=P),
         )
+        x_halves[4] = load_x_half(4, 1)
         beta = consts.tile([P, TILES * WIDTH], BF16)
         nc.sync.dma_start(
             out=beta[:].rearrange("p (it j) -> p it j", it=TILES),
             in_=beta_o.rearrange("(it p) j -> p it j", p=P),
         )
-        for h in range(3, X_AHEAD):
-            x_halves[h] = load_x_half(h, 1)
+        x_halves[5] = load_x_half(5, 1)
+        gamma_sum = consts.tile([P, WIDTH], BF16)
+        nc.sync.dma_start(out=gamma_sum[0:BATCH, :], in_=gamma_o_sum.partition_broadcast(BATCH))
+        beta_sum = consts.tile([P, WIDTH], BF16)
+        nc.sync.dma_start(out=beta_sum[0:BATCH, :], in_=beta_o_sum.partition_broadcast(BATCH))
 
         identity = consts.tile([P, P], F32)
         make_identity(nc, identity[:])
@@ -360,6 +363,8 @@ def tile_selfprojection_pa_kernel(
 
         def st_xi():
             quantise_weight(xi_raw, xi_codes, xi_scales)
+
+        def st_beta_sum():
             nc.vector.tensor_scalar_add(
                 out=beta_sum_plus_1[c_rows, :], in0=beta_sum[c_rows, :], scalar1=1.0
             )
@@ -547,7 +552,7 @@ def tile_selfprojection_pa_kernel(
             nc.sync.dma_start(out=out_1[:, :], in_=o_sum[c_rows, :])
 
         stages = {
-            "load": st_load, "xj": st_xj, "xi": st_xi, "tp": st_tp, "to": st_to, "qx": st_qx,
+            "load": st_load, "xj": st_xj, "xi": st_xi, "beta_sum": st_beta_sum, "tp": st_tp, "to": st_to, "qx": st_qx,
             "m1p": st_m1p, "m1o": st_m1o, "dup": st_dup, "add": st_add, "qy": st_qy,
             "m2p": st_m2p, "m2o": st_m2o, "meanp": st_meanp, "meana": st_meana, "sq": st_sq,
             "sel": st_sel, "stt1": st_stt1, "stdp": st_stdp, "stda": st_stda, "inv": st_inv,

from contextlib import ExitStack

import concourse.mybir as mybir
from concourse.masks import make_identity

F32 = mybir.dt.float32
BF16 = mybir.dt.bfloat16
U32 = mybir.dt.uint32
U8 = mybir.dt.uint8
FP8X4 = mybir.dt.float8_e4m3fn_x4
ACT = mybir.ActivationFunctionType
ALU = mybir.AluOpType
AXIS = mybir.AxisListType

BATCH = 6
ROWS = 1024
INNER = 1024
WIDTH = 512
EPS = 1e-05

P = 128
PACK = 4
K_PASS = P * PACK
PASSES = 2
BANK = 512
TILES = WIDTH // P
HALVES = BATCH * PASSES
X_AHEAD = 6
FIRST_LOAD_PIECES = 4
PIECES = 2
PIECE = TILES * WIDTH // PIECES

SECOND_MATMUL_STEP = 2
MEAN_STEP = 3
STD_STEP = 4
BIAS_STEP = 5
LAST_STEP = BIAS_STEP + 2 * (BATCH - 1)

FLOPS = BATCH * (2 * ROWS * INNER * WIDTH + 2 * ROWS * WIDTH * WIDTH)


def batch_at(step, first_step):
    b, rest = divmod(step - first_step, PASSES)
    return b if rest == 0 and 0 <= b < BATCH else None


VEC_X = (1, 2, 3, 4, 5, 6, 7, 8, 9)


def program():
    prog = [("xj",)]
    last = HALVES - 1
    for step in range(-1, last):
        b_second = batch_at(step, SECOND_MATMUL_STEP)
        b_mean = batch_at(step, MEAN_STEP)
        b_std = batch_at(step, STD_STEP)
        coming = step + 1
        b, g = divmod(step, PASSES)
        for t in range(PACK):
            prog.append(("tp", coming, t))
            prog.append(("to", coming, t, t == 0 and step in VEC_X))
        if coming + X_AHEAD < HALVES:
            prog.append(("load", coming + X_AHEAD))
        if step == 1:
            prog.append(("xi",))
        if step == 3:
            prog.append(("beta_sum",))
        if b_mean is not None:
            prog.extend([("meanp", b_mean), ("meana", b_mean)])
        if b_std is not None:
            prog.append(("stdp", b_std))
        for t in range(PACK):
            prog.append(("qx", coming, t, 1))
        if b_mean is not None:
            prog.extend([("stt1", b_mean, 0, 2), ("stt1", b_mean, 2, 2)])
        if step >= 0:
            for jc in range(TILES):
                prog.append(("m1p", step, jc))
                prog.append(("m1o", step, jc, False, g == 0))
            if g == 1:
                prog.append(("dup", step, True, True))
        if b_std is not None:
            prog.extend([("stda", b_std), ("inv", b_std)])
        if step >= 0:
            prog.append(("qy", step))
            if g == 1:
                prog.append(("add", b))
        if b_std is not None:
            prog.extend([("stt2", b_std, 0, 2), ("stt2", b_std, 2, 2)])
        if b_second is not None:
            for it in range(TILES):
                prog.extend([("m2p", b_second, it), ("m2o", b_second, it)])
        if b_mean is not None:
            prog.append(("sq", b_mean))
    b4, b5 = BATCH - 2, BATCH - 1
    prog.extend([("m1p", last, jc) for jc in range(TILES)])
    prog.extend([("meanp", b4), ("meana", b4), ("dup", last, True, True)])
    prog.extend([("sel", 0), ("sel", 1)])
    prog.append(("stt1", b4, 0, 2))
    prog.extend([("m1o", last, jc, False, False) for jc in range(TILES)])
    prog.extend([("qy", last), ("stt1", b4, 2, 2), ("add", b5)])
    prog.extend([("m2p", b5, 0), ("m2p", b5, 1), ("sq", b4), ("stdp", b4), ("m2p", b5, 2), ("m2p", b5, 3)])
    prog.extend([("m2o", b5, 0), ("stda", b4), ("m2o", b5, 1), ("m2o", b5, 2), ("m2o", b5, 3)])
    prog.extend([("sel", 2), ("sel", 3)])
    prog.extend([("inv", b4), ("stt2", b4, 0, 2), ("stt2", b4, 2, 2)])
    prog.extend([("meanp", b5), ("meana", b5), ("sq", b5), ("sel", 4), ("sel", 5)])
    prog.extend([("stt1", b5, 0, 2), ("stt1", b5, 2, 2)])
    prog.extend([("stdp", b5), ("stda", b5), ("inv", b5)])
    prog.extend([("c_stats",), ("c_std",)])
    prog.extend([("stt2", b5, 0, 2), ("stt2", b5, 2, 2), ("c_out",)])
    return prog


def tile_selfprojection_pa_kernel(
    tc,
    x,
    original_xj_y,
    original_xi_y,
    gamma_o_sum,
    gamma_o,
    beta_o_sum,
    beta_o,
    out_0,
    out_1,
):
    nc = tc.nc
    with ExitStack() as ctx:
        consts = ctx.enter_context(tc.tile_pool(name="consts", bufs=1))
        weights = ctx.enter_context(tc.tile_pool(name="weights", bufs=2))
        x_pool = ctx.enter_context(tc.tile_pool(name="x_pool", bufs=X_AHEAD))
        work = ctx.enter_context(tc.tile_pool(name="work", bufs=2))
        small = ctx.enter_context(tc.tile_pool(name="small", bufs=2))
        kept = ctx.enter_context(tc.tile_pool(name="kept", bufs=BATCH))
        psum = ctx.enter_context(tc.psum_pool(name="psum", bufs=8))
        ctx.enter_context(tc.manual_schedule())

        def load_x_half(h, pieces):
            b, g = divmod(h, PASSES)
            x_half = x_pool.tile([P, PACK * INNER], BF16)
            row_groups = x[b].rearrange("(g p t) n -> g p t n", g=PASSES, p=P, t=PACK)
            in_sbuf = x_half[:].rearrange("p (t n) -> p t n", t=PACK)
            per_piece = PACK // pieces
            for first in range(0, PACK, per_piece):
                nc.sync.dma_start(
                    out=in_sbuf[:, first : first + per_piece, :],
                    in_=row_groups[g][:, first : first + per_piece, :],
                )
            return x_half

        def load_weight(in_word_order):
            raw = weights.tile([P, PASSES * PACK * WIDTH], BF16)
            for s in range(PASSES):
                nc.sync.dma_start(
                    out=raw[:, s * PACK * WIDTH : (s + 1) * PACK * WIDTH].rearrange(
                        "p (u e w) -> p u e w", u=2, e=2
                    ),
                    in_=in_word_order[s],
                )
            return raw

        xj_raw = load_weight(
            original_xj_y.rearrange("(c u q e) j -> c q u e j", c=PASSES, u=2, q=P, e=2)
        )
        x_halves = {
            0: load_x_half(0, FIRST_LOAD_PIECES),
            1: load_x_half(1, FIRST_LOAD_PIECES),
            2: load_x_half(2, 1),
        }
        xi_raw = load_weight(
            original_xi_y.rearrange("(g p u e) i -> g p u e i", g=PASSES, p=P, u=2, e=2)
        )
        x_halves[3] = load_x_half(3, 1)
        gamma = consts.tile([P, TILES * WIDTH], BF16)
        nc.sync.dma_start(
            out=gamma[:].rearrange("p (it j) -> p it j", it=TILES),
            in_=gamma_o.rearrange("(it p) j -> p it j", p=P),
        )
        x_halves[4] = load_x_half(4, 1)
        beta = consts.tile([P, TILES * WIDTH], BF16)
        nc.sync.dma_start(
            out=beta[:].rearrange("p (it j) -> p it j", it=TILES),
            in_=beta_o.rearrange("(it p) j -> p it j", p=P),
        )
        x_halves[5] = load_x_half(5, 1)
        gamma_sum = consts.tile([P, WIDTH], BF16)
        nc.sync.dma_start(out=gamma_sum[0:BATCH, :], in_=gamma_o_sum.partition_broadcast(BATCH))
        beta_sum = consts.tile([P, WIDTH], BF16)
        nc.sync.dma_start(out=beta_sum[0:BATCH, :], in_=beta_o_sum.partition_broadcast(BATCH))

        identity = consts.tile([P, P], F32)
        make_identity(nc, identity[:])
        ones = consts.tile([P, P], F32)
        nc.gpsimd.memset(ones[:], 1.0)
        neg_average = consts.tile([P, P], F32)
        nc.gpsimd.memset(neg_average[:], -1.0 / (WIDTH * WIDTH))
        selectors = consts.tile([P, BATCH * P], F32)
        nc.gpsimd.memset(selectors[:], 0.0)
        for b in range(BATCH):
            nc.gpsimd.memset(selectors[:, b * P + b : b * P + b + 1], 1.0)
        one = consts.tile([P, 1], F32)
        nc.vector.memset(one[:], 1.0)
        sqrt_of_one = consts.tile([P, 1], F32)
        nc.scalar.activation(out=sqrt_of_one[:], in_=one[:], func=ACT.Sqrt)

        def quantise_weight(raw, codes, scales):
            grouped = weights.tile([P, PASSES * PACK * WIDTH], BF16, align_bytes=64)
            for s in range(PASSES):
                cols = slice(s * PACK * WIDTH, (s + 1) * PACK * WIDTH)
                nc.vector.tensor_copy(
                    out=grouped[:, cols].rearrange("p (w i t) -> p w t i", i=4, t=PACK),
                    in_=raw[:, cols].rearrange("p (t w i) -> p w t i", t=PACK, i=4),
                )
            nc.vector.quantize_mx(out=codes[:].bitcast(FP8X4), scales=scales[:], in_=grouped[:])

        xj_codes = consts.tile([P, PASSES * WIDTH], U32, align_bytes=64)
        xj_scales = consts.tile([P, PASSES * WIDTH], U8, align_bytes=64)
        xi_codes = consts.tile([P, PASSES * WIDTH], U32, align_bytes=64)
        xi_scales = consts.tile([P, PASSES * WIDTH], U8, align_bytes=64)

        def transpose_x_rows(x_half, t):
            words = x_half[:].bitcast(F32)
            bank = psum.tile([P, BANK], F32, tag="bank")
            for cu in range(BANK // P):
                first = t * (INNER // 2) + cu * P
                nc.tensor.transpose(
                    bank[:, cu * P : (cu + 1) * P], words[:, first : first + P], identity[:]
                )
            return bank

        def copy_x_rows(bank, t, x_grouped, copy_on_vector):
            grouped_words = x_grouped[:].bitcast(F32).rearrange(
                "q (t c m u) -> q t c m u", t=PACK, c=PASSES, m=P, u=2
            )
            side_by_side = bank[:].rearrange("q (c u m) -> q c m u", c=PASSES, u=2, m=P)
            if copy_on_vector:
                nc.vector.tensor_copy(out=grouped_words[:, t, :, :, :], in_=side_by_side)
            else:
                nc.scalar.copy(out=grouped_words[:, t, :, :, :], in_=side_by_side)

        def quantise_x_rows(x_grouped, x_codes, x_scales, t_first, t_count):
            word_cols = slice(t_first * PASSES * P, (t_first + t_count) * PASSES * P)
            nc.vector.quantize_mx(
                out=x_codes[:, word_cols].bitcast(FP8X4),
                scales=x_scales[:, word_cols],
                in_=x_grouped[:, t_first * PASSES * P * PACK : (t_first + t_count) * PASSES * P * PACK],
            )

        def first_matmul(jc, x_codes, x_scales):
            bank = psum.tile([P, BANK], F32, tag="bank")
            for t in range(PACK):
                for c in range(PASSES):
                    m_cols = slice((t * PASSES + c) * P, (t * PASSES + c + 1) * P)
                    j_cols = slice(c * WIDTH + jc * P, c * WIDTH + (jc + 1) * P)
                    nc.tensor.matmul_mx(
                        out=bank[:, t * P : (t + 1) * P],
                        lhsT=x_codes[:, m_cols].bitcast(FP8X4),
                        lhsT_scale=x_scales[:, m_cols],
                        rhs=xj_codes[:, j_cols].bitcast(FP8X4),
                        rhs_scale=xj_scales[:, j_cols],
                        start=(c == 0),
                        stop=(c == PASSES - 1),
                    )
            return bank

        def copy_y(bank, jc, y_grouped, half_sums, copy_on_vector):
            by_column = bank[:].rearrange("p (t j) -> p j t", t=PACK)
            y_out = y_grouped[:, jc * BANK : (jc + 1) * BANK].rearrange("p (j t) -> p j t", t=PACK)
            if copy_on_vector:
                nc.vector.tensor_copy(out=y_out, in_=by_column)
            else:
                nc.scalar.copy(out=y_out, in_=by_column)
            if half_sums is not None:
                nc.vector.tensor_reduce(
                    out=half_sums[:, jc * P : (jc + 1) * P], in_=by_column, axis=AXIS.X, op=ALU.add
                )

        def add_rows_in_psum(bank, opens, closes, x_codes, x_scales):
            for t in range(PACK):
                for c in range(PASSES):
                    m_cols = slice((t * PASSES + c) * P, (t * PASSES + c + 1) * P)
                    j_cols = slice(c * WIDTH, (c + 1) * WIDTH)
                    nc.tensor.matmul_mx(
                        out=bank[:],
                        lhsT=x_codes[:, m_cols].bitcast(FP8X4),
                        lhsT_scale=x_scales[:, m_cols],
                        rhs=xj_codes[:, j_cols].bitcast(FP8X4),
                        rhs_scale=xj_scales[:, j_cols],
                        start=(opens and t == 0 and c == 0),
                        stop=(closes and t == PACK - 1 and c == PASSES - 1),
                    )

        def second_matmul(it, y_codes, y_scales):
            bank = psum.tile([P, BANK], F32, tag="bank")
            for g in range(PASSES):
                i_cols = slice(g * WIDTH + it * P, g * WIDTH + (it + 1) * P)
                j_cols = slice(g * WIDTH, (g + 1) * WIDTH)
                nc.tensor.matmul_mx(
                    out=bank[:],
                    lhsT=xi_codes[:, i_cols].bitcast(FP8X4),
                    lhsT_scale=xi_scales[:, i_cols],
                    rhs=y_codes[:, j_cols].bitcast(FP8X4),
                    rhs_scale=y_scales[:, j_cols],
                    start=(g == 0),
                    stop=(g == PASSES - 1),
                )
            return bank

        def copy_z(bank, it, z, row_sums):
            nc.scalar.activation(
                out=z[:, it * WIDTH : (it + 1) * WIDTH],
                in_=bank[:],
                func=ACT.Copy,
                accum_out=row_sums[:, it : it + 1],
            )

        def totals_over_partitions(weight, parts):
            bank = psum.tile([P, BANK], F32, tag="bank")
            totals = bank[:, 0 : parts.shape[1]]
            nc.tensor.matmul(out=totals, lhsT=weight[:], rhs=parts[:], start=True, stop=True)
            return totals

        def std_of(rows, sum_or_variance, scale):
            std = small.tile([P, 1], F32)
            nc.scalar.activation(
                out=std[rows, :], in_=sum_or_variance, func=ACT.Sqrt, scale=scale
            )
            return std

        def one_over(rows, std):
            std_eps = small.tile([P, 1], F32)
            nc.vector.tensor_scalar_add(out=std_eps[rows, :], in0=std[rows, :], scalar1=EPS)
            inverse = small.tile([P, 1], F32)
            nc.vector.reciprocal(out=inverse[rows, :], in_=std_eps[rows, :])
            return inverse

        all_rows = slice(0, P)
        c_rows = slice(0, BATCH)
        beta_sum_plus_1 = consts.tile([P, WIDTH], F32)
        c_mean_var = consts.tile([P, 2], F32)
        c_bank = psum.tile([P, BANK], F32, tag="bank")
        x_raw = {}
        x_mx = {}
        y_raw = {}
        y_mx = {}
        column_sums = {}
        psum_sums = {}
        batch_sums = {}
        z = {}
        row_sums = {}
        neg_mean = {}
        square_sums = {}
        scaled = {}
        stds = {}
        inverse_std = {}
        selected = []
        banks = {}

        def st_load(h):
            x_halves[h] = load_x_half(h, 1)

        def st_xj():
            quantise_weight(xj_raw, xj_codes, xj_scales)

        def st_xi():
            quantise_weight(xi_raw, xi_codes, xi_scales)

        def st_beta_sum():
            nc.vector.tensor_scalar_add(
                out=beta_sum_plus_1[c_rows, :], in0=beta_sum[c_rows, :], scalar1=1.0
            )

        def st_tp(h, t):
            banks["t", h, t] = transpose_x_rows(x_halves[h], t)

        def st_to(h, t, on_vector):
            if h not in x_raw:
                x_grouped = work.tile([P, PASSES * PACK * P * PACK], BF16, align_bytes=64)
                x_raw[h] = x_grouped
            copy_x_rows(banks["t", h, t], t, x_raw[h], on_vector)

        def st_qx(h, t_first, t_count):
            if h not in x_mx:
                x_codes = work.tile([P, PACK * PASSES * P], U32, align_bytes=64)
                x_scales = work.tile([P, PACK * PASSES * P], U8, align_bytes=64)
                x_mx[h] = (x_codes, x_scales)
            quantise_x_rows(x_raw[h], x_mx[h][0], x_mx[h][1], t_first, t_count)

        def st_m1p(h, jc):
            banks["y", h, jc] = first_matmul(jc, x_mx[h][0], x_mx[h][1])

        def st_m1o(h, jc, on_vector, reduce_on_vector):
            b, g = divmod(h, PASSES)
            if h not in y_raw:
                y_grouped = work.tile([P, WIDTH * PACK], BF16, align_bytes=64)
                y_raw[h] = y_grouped
            if reduce_on_vector and b not in column_sums:
                sums = work.tile([P, WIDTH], F32)
                column_sums[b] = sums
            copy_y(banks["y", h, jc], jc, y_raw[h], column_sums[b] if reduce_on_vector else None, on_vector)

        def st_dup(h, opens, closes):
            b = h // PASSES
            if opens:
                sum_bank = psum.tile([P, BANK], F32, tag="bank")
                psum_sums[b] = sum_bank
            add_rows_in_psum(psum_sums[b], opens, closes, x_mx[h][0], x_mx[h][1])

        def st_add(b):
            sums_of_batch = kept.tile([P, WIDTH], F32)
            batch_sums[b] = sums_of_batch
            if b in column_sums:
                nc.vector.tensor_tensor(
                    out=sums_of_batch[:], in0=psum_sums[b][:], in1=column_sums[b][:], op=ALU.add
                )
            else:
                nc.vector.tensor_copy(out=sums_of_batch[:], in_=psum_sums[b][:])

        def st_qy(h):
            b, g = divmod(h, PASSES)
            if b not in y_mx:
                y_codes = work.tile([P, PASSES * WIDTH], U32, align_bytes=64)
                y_scales = work.tile([P, PASSES * WIDTH], U8, align_bytes=64)
                y_mx[b] = (y_codes, y_scales)
            pass_cols = slice(g * WIDTH, (g + 1) * WIDTH)
            nc.vector.quantize_mx(
                out=y_mx[b][0][:, pass_cols].bitcast(FP8X4),
                scales=y_mx[b][1][:, pass_cols],
                in_=y_raw[h][:],
            )

        def st_m2p(b, it):
            banks["z", b, it] = second_matmul(it, y_mx[b][0], y_mx[b][1])

        def st_m2o(b, it):
            if b not in z:
                z_tile = work.tile([P, TILES * WIDTH], F32)
                z[b] = z_tile
                z_row_sums = small.tile([P, TILES], F32)
                row_sums[b] = z_row_sums
            copy_z(banks["z", b, it], it, z[b], row_sums[b])

        def st_meanp(b):
            banks["mean", b] = totals_over_partitions(neg_average, row_sums[b])

        def st_meana(b):
            minus_mean = small.tile([P, 1], F32)
            tile_means = small.tile([P, TILES], F32)
            nc.scalar.activation(
                out=tile_means[:], in_=banks["mean", b], func=ACT.Copy, accum_out=minus_mean[:]
            )
            neg_mean[b] = minus_mean

        def st_sq(b):
            squares = work.tile([P, TILES * WIDTH], BF16)
            z_square_sums = small.tile([P, 1], F32)
            square_sums[b] = z_square_sums
            nc.scalar.activation(
                out=squares[:],
                in_=z[b][:],
                func=ACT.Square,
                bias=neg_mean[b][:],
                accum_out=z_square_sums[:],
            )

        def st_sel(b):
            selected.append(b)
            nc.tensor.matmul(
                out=c_bank[:],
                lhsT=selectors[:, b * P : (b + 1) * P],
                rhs=batch_sums[b][:],
                start=(len(selected) == 1),
                stop=(len(selected) == BATCH),
            )

        def st_stt1(b, first, count):
            if b not in scaled:
                gained = work.tile([P, TILES * WIDTH], F32)
                scaled[b] = gained
            cols = slice(first * WIDTH, (first + count) * WIDTH)
            nc.vector.scalar_tensor_tensor(
                out=scaled[b][:, cols],
                in0=z[b][:, cols],
                scalar=neg_mean[b][:],
                in1=gamma[:, cols],
                op0=ALU.add,
                op1=ALU.mult,
            )

        def st_stdp(b):
            banks["std", b] = totals_over_partitions(ones, square_sums[b])

        def st_stda(b):
            stds[b] = std_of(all_rows, banks["std", b], 1.0 / (WIDTH * WIDTH - 1))

        def st_inv(b):
            inverse_std[b] = one_over(all_rows, stds[b])

        def st_stt2(b, first, count):
            cols = slice(first * WIDTH, (first + count) * WIDTH)
            nc.vector.scalar_tensor_tensor(
                out=scaled[b][:, cols],
                in0=scaled[b][:, cols],
                scalar=inverse_std[b][:],
                in1=beta[:, cols],
                op0=ALU.mult,
                op1=ALU.add,
            )
            nc.sync.dma_start(
                out=out_0[b, first * P : (first + count) * P, :].rearrange("(it p) j -> p it j", p=P),
                in_=scaled[b][:, cols].rearrange("p (it j) -> p it j", j=WIDTH),
            )

        def st_c_stats():
            c_junk = work.tile([P, WIDTH], BF16)
            nc.scalar.activation(
                out=c_junk[c_rows, :],
                in_=c_bank[c_rows, :],
                func=ACT.Copy,
                scale=-1.0 / WIDTH,
                accum_out=c_mean_var[c_rows, 0:1],
            )
            nc.scalar.activation(
                out=c_junk[c_rows, :],
                in_=c_bank[c_rows, :],
                func=ACT.Square,
                bias=c_mean_var[c_rows, 0:1],
                accum_out=c_mean_var[c_rows, 1:2],
            )

        def st_c_std():
            stds[BATCH] = std_of(c_rows, c_mean_var[c_rows, 1:2], 1.0 / (WIDTH - 1.0))

        def st_c_out():
            c_inverse_std = one_over(c_rows, stds[BATCH])
            o_sum = work.tile([P, WIDTH], F32)
            nc.vector.scalar_tensor_tensor(
                out=o_sum[c_rows, :],
                in0=c_bank[c_rows, :],
                scalar=c_mean_var[c_rows, 0:1],
                in1=gamma_sum[c_rows, :],
                op0=ALU.add,
                op1=ALU.mult,
            )
            nc.vector.scalar_tensor_tensor(
                out=o_sum[c_rows, :],
                in0=o_sum[c_rows, :],
                scalar=c_inverse_std[c_rows, :],
                in1=beta_sum_plus_1[c_rows, :],
                op0=ALU.mult,
                op1=ALU.add,
            )
            nc.sync.dma_start(out=out_1[:, :], in_=o_sum[c_rows, :])

        stages = {
            "load": st_load, "xj": st_xj, "xi": st_xi, "beta_sum": st_beta_sum, "tp": st_tp, "to": st_to, "qx": st_qx,
            "m1p": st_m1p, "m1o": st_m1o, "dup": st_dup, "add": st_add, "qy": st_qy,
            "m2p": st_m2p, "m2o": st_m2o, "meanp": st_meanp, "meana": st_meana, "sq": st_sq,
            "sel": st_sel, "stt1": st_stt1, "stdp": st_stdp, "stda": st_stda, "inv": st_inv,
            "stt2": st_stt2, "c_stats": st_c_stats, "c_std": st_c_std, "c_out": st_c_out,
        }
        for entry in program():
            stages[entry[0]](*entry[1:])
